import numpy as np
import ml_dtypes


def mxq(x, axis, fmt="e4m3"):
    dtype, down = {"e4m3": (ml_dtypes.float8_e4m3fn, 7), "e5m2": (ml_dtypes.float8_e5m2, 14)}[fmt]
    v = np.moveaxis(np.asarray(x, np.float32).astype(ml_dtypes.bfloat16).astype(np.float64), axis, -1)
    blocks = v.reshape(v.shape[:-1] + (-1, 32))
    amax = np.abs(blocks).max(-1, keepdims=True)
    byte = np.maximum(np.where(amax > 0, np.frexp(amax)[1] - 1 + 127, 0) - down, 1)
    scale = np.exp2(byte - 127.0)
    codes = (blocks / scale).astype(np.float32).astype(dtype).astype(np.float64)
    return np.moveaxis((codes * scale).reshape(v.shape), -1, axis)


WIDE = False


def mx_kscale(k):
    if not WIDE:
        return np.ones(k)
    levels = np.array([10, -10, 5, -5, 0])
    a = np.random.permutation(np.resize(levels, k // 512 * 4)).reshape(k // 512, 4)
    idx = np.arange(k)
    return np.exp2(a[idx // 512, idx % 128 // 32])


BF16 = ml_dtypes.bfloat16


def bf(x):
    return np.asarray(x, np.float32).astype(BF16)


def f64(x):
    return np.asarray(x).astype(np.float64)


E2M1 = np.array([0.0, 0.5, 1.0, 1.5, 2.0, 3.0, 4.0, 6.0, -0.0, -0.5, -1.0, -1.5, -2.0, -3.0, -4.0, -6.0])


def pack_weight(w, fmt):
    k, n = w.shape
    w = f64(bf(w)).reshape(k // 32, 32, n)
    amax = np.abs(w).max(1)
    if fmt == "e4m3":
        byte = np.frexp(amax)[1] - 1 + 127 - 7
    else:
        mant, ex = np.frexp(amax / 6.0)
        byte = np.where(mant > 0.5, ex, ex - 1) + 127
    byte = np.clip(np.where(amax > 0, byte, 1), 1, 254)
    scaled = (w * np.exp2(127.0 - byte)[:, None, :]).reshape(k, n).astype(np.float32)
    by_word = np.ascontiguousarray(scaled.reshape(k // 512, 128, 4, n).transpose(0, 1, 3, 2))
    if fmt == "e4m3":
        words = by_word.astype(ml_dtypes.float8_e4m3fn).view(np.uint8)
    else:
        c = by_word.astype(ml_dtypes.float4_e2m1fn).view(np.uint8) & 0xF
        words = c[..., 0::2] | (c[..., 1::2] << 4)
    return np.ascontiguousarray(words), np.ascontiguousarray(byte.astype(np.uint8).reshape(k // 512, 16, n))


def unpack_weight(words, scales, fmt):
    g, p, n, _ = words.shape
    if fmt == "e4m3":
        vals = np.ascontiguousarray(words).view(ml_dtypes.float8_e4m3fn).astype(np.float64)
    else:
        nib = np.empty((g, p, n, 4), np.uint8)
        nib[..., 0::2] = words & 0xF
        nib[..., 1::2] = words >> 4
        vals = E2M1[nib]
    vals = vals * np.repeat(np.exp2(scales.astype(np.float64) - 127.0), 8, axis=1)[..., None]
    return vals.transpose(0, 1, 3, 2).reshape(g * 512, n)


B, DIM, D2, T = 1, 512, 1024, 512


def setup_inputs():
    s = mx_kscale(D2)
    es = 0.25 * s[None, :, None]
    ws = 0.35 / np.sqrt(D2) / s[:, None] / s[None, :]
    E_re = bf(np.random.standard_normal((B, D2, T)) * es)
    E_im = bf(np.random.standard_normal((B, D2, T)) * es)
    re_words, re_scales = pack_weight((np.random.standard_normal((D2, D2)) * ws).T, "e4m3")
    im_words, im_scales = pack_weight((np.random.standard_normal((D2, D2)) * ws).T, "e4m3")
    return {"E_re": E_re,
            "E_im": E_im,
            "WKQ_re_words": re_words, "WKQ_re_scales": re_scales,
            "WKQ_im_words": im_words, "WKQ_im_scales": im_scales}


def reference(E_re, E_im, WKQ_re_words, WKQ_re_scales, WKQ_im_words, WKQ_im_scales):
    er = mxq(f64(E_re), 1, "e4m3")
    ei = mxq(f64(E_im), 1, "e4m3")
    wr = unpack_weight(WKQ_re_words, WKQ_re_scales, "e4m3").T
    wi = unpack_weight(WKQ_im_words, WKQ_im_scales, "e4m3").T
    q_re = (wr @ er) - (wi @ ei)
    q_im = (wr @ ei) + (wi @ er)
    qr = mxq(q_re, 1, "e4m3")
    qi = mxq(q_im, 1, "e4m3")
    ert = er.transpose(0, 2, 1)
    eit = ei.transpose(0, 2, 1)
    s_re = (ert @ qr) + (eit @ qi)
    s_im = (ert @ qi) - (eit @ qr)
    return s_re, s_im

@@ -1,0 +1,225 @@
+from contextlib import ExitStack
+
+import concourse.mybir as mybir
+
+FP8X4 = mybir.dt.float8_e4m3fn_x4
+BF16 = mybir.dt.bfloat16
+F32 = mybir.dt.float32
+I32 = mybir.dt.int32
+U32 = mybir.dt.uint32
+U8 = mybir.dt.uint8
+
+P = 128
+PACK = 4
+K_PASS = P * PACK
+CHANNELS = 1024
+POSITIONS = 512
+PASSES = CHANNELS // K_PASS
+M_TILE = 128
+HALF = PACK * M_TILE
+RUN = 4
+BANKS = 8
+
+FLOPS = 2 * 4 * (CHANNELS * CHANNELS * POSITIONS + POSITIONS * CHANNELS * POSITIONS)
+
+PARTS = ("re", "im")
+
+Q_TERMS = {"re": (("re", "re"), ("im", "neg_im")), "im": (("im", "re"), ("re", "im"))}
+S_OPERAND = {("re", "re"): "re", ("re", "im"): "im", ("im", "re"): "neg_im", ("im", "im"): "re"}
+
+
+def mx_operand(pool, name, passes, columns):
+    return {
+        "grouped": pool.tile([P, passes, columns, PACK], BF16, name=name + "_grouped", align_bytes=64),
+        "words": pool.tile([P, passes, columns], U32, name=name + "_words", align_bytes=64),
+        "scales": pool.tile([P, passes, columns], U8, name=name + "_scales", align_bytes=64),
+    }
+
+
+def regroup_views(grouped, rows):
+    return (
+        grouped.rearrange("p (c i) j -> p c j i", i=RUN),
+        rows.rearrange("p j (c i) -> p c j i", i=RUN),
+    )
+
+
+def quantise(nc, operand, g):
+    nc.vector.quantize_mx(
+        out=operand["words"][:, g, :].bitcast(FP8X4),
+        scales=operand["scales"][:, g, :],
+        in_=operand["grouped"][:, g, :, :].rearrange("p w j -> p (w j)"),
+    )
+
+
+def tile_autoregressivelsa_pa_kernel(
+    tc, E_re, E_im, WKQ_re_words, WKQ_re_scales, WKQ_im_words, WKQ_im_scales, out_0, out_1
+):
+    nc = tc.nc
+    e_dram = {"re": E_re.flatten_outer_dims(), "im": E_im.flatten_outer_dims()}
+    w_words_dram = {"re": WKQ_re_words, "im": WKQ_im_words}
+    w_scales_dram = {"re": WKQ_re_scales, "im": WKQ_im_scales}
+    s_dram = {"re": out_0.flatten_outer_dims(), "im": out_1.flatten_outer_dims()}
+
+    with ExitStack() as ctx:
+        keep = ctx.enter_context(tc.tile_pool(name="keep", bufs=1))
+        banks = ctx.enter_context(tc.psum_pool(name="banks", bufs=BANKS))
+        ctx.enter_context(tc.manual_schedule())
+
+        w_words = {w: keep.tile([P, PASSES, CHANNELS], U32, name="w_words_" + w, align_bytes=64) for w in PARTS}
+        w_scales = keep.tile([P, CHANNELS], U8, name="w_scales", align_bytes=64)
+        w_plane = {(w, g): PACK * (PASSES * PARTS.index(w) + g) for w in PARTS for g in range(PASSES)}
+
+        e_rows = {}
+        e_mx = {}
+        for order in ("by4", "by128"):
+            for part in PARTS:
+                e_rows[order, part] = keep.tile(
+                    [P, PASSES, PACK, POSITIONS], BF16, name="e_rows_%s_%s" % (order, part)
+                )
+            for operand in ("re", "im", "neg_im"):
+                e_mx[order, operand] = mx_operand(keep, "e_%s_%s" % (order, operand), PASSES, POSITIONS)
+        q_rows = {part: keep.tile([P, PASSES, PACK, POSITIONS], BF16, name="q_rows_" + part) for part in PARTS}
+        q_mx = {part: mx_operand(keep, "q_" + part, PASSES, POSITIONS) for part in PARTS}
+
+        def load_e(order, part, g):
+            rows = e_dram[part][K_PASS * g : K_PASS * (g + 1), :]
+            if order == "by4":
+                view = rows.rearrange("(p j) t -> p j t", j=PACK)
+            else:
+                view = rows.rearrange("(j p) t -> p j t", p=P)
+            nc.sync.dma_start(out=e_rows[order, part][:, g, :, :], in_=view)
+
+        def load_w_words(w, g, half):
+            cols = slice(HALF * half, HALF * (half + 1))
+            byte_cols = slice(PACK * HALF * half, PACK * HALF * (half + 1))
+            nc.sync.dma_start(
+                out=w_words[w][:, g, cols].bitcast(I32),
+                in_=w_words_dram[w][g].rearrange("p n t -> p (n t)")[:, byte_cols].bitcast(I32),
+            )
+
+        def load_w_scales(w):
+            first = w_plane[w, 0]
+            for quadrant in range(4):
+                nc.sync.dma_start(
+                    out=w_scales[32 * quadrant + first : 32 * quadrant + first + PACK * PASSES, :].bitcast(I32),
+                    in_=w_scales_dram[w][:, 4 * quadrant : 4 * quadrant + 4, :].bitcast(I32),
+                )
+
+        nc.vector.memset(w_scales[:].bitcast(I32), 0)
+        load_e("by4", "re", 0)
+        for w in PARTS:
+            load_w_scales(w)
+            load_w_words(w, 0, 0)
+        load_e("by4", "im", 0)
+        load_e("by4", "re", 1)
+        for w in PARTS:
+            load_w_words(w, 1, 0)
+        load_e("by4", "im", 1)
+        load_e("by128", "im", 0)
+        for g in range(PASSES):
+            for w in PARTS:
+                load_w_words(w, g, 1)
+        load_e("by128", "re", 0)
+        load_e("by128", "re", 1)
+        load_e("by128", "im", 1)
+
+        def regroup_e(copy, order, operand, part, g):
+            dst, src = regroup_views(e_mx[order, operand]["grouped"][:, g, :, :], e_rows[order, part][:, g, :, :])
+            copy(dst, src)
+
+        def vector_copy(dst, src):
+            nc.vector.tensor_copy(out=dst, in_=src)
+
+        def vector_negate(dst, src):
+            nc.vector.tensor_scalar_mul(out=dst, in0=src, scalar1=-1.0)
+
+        def scalar_copy(dst, src):
+            nc.scalar.copy(out=dst, in_=src)
+
+        def regroup_q(part, half):
+            dst, src = regroup_views(q_mx[part]["grouped"][:, half, :, :], q_rows[part][:, half, :, :])
+            nc.vector.tensor_copy(out=dst, in_=src)
+
+        def q_pass(acc, part, term, g, m):
+            w, operand = Q_TERMS[part][term]
+            cols = slice(M_TILE * m, M_TILE * (m + 1))
+            nc.tensor.matmul_mx(
+                out=acc[:],
+                lhsT=w_words[w][:, g, cols].bitcast(FP8X4),
+                lhsT_scale=w_scales[w_plane[w, g] : P, cols],
+                rhs=e_mx["by4", operand]["words"][:, g, :].bitcast(FP8X4),
+                rhs_scale=e_mx["by4", operand]["scales"][:, g, :],
+                start=(g == 0 and term == 0),
+                stop=(g == PASSES - 1 and term == 1),
+            )
+
+        acc0 = {
+            (part, j): banks.tile([P, POSITIONS], F32, name="acc", tag="acc") for part in PARTS for j in range(PACK)
+        }
+        for g in range(PASSES):
+            regroup_e(vector_copy, "by4", "re", "re", g)
+            quantise(nc, e_mx["by4", "re"], g)
+            regroup_e(scalar_copy, "by4", "im", "im", g)
+            regroup_e(vector_negate, "by4", "neg_im", "im", g)
+            quantise(nc, e_mx["by4", "neg_im"], g)
+            quantise(nc, e_mx["by4", "im"], g)
+            for term in range(2):
+                for part in PARTS:
+                    for j in range(PACK):
+                        q_pass(acc0[part, j], part, term, g, j)
+
+        regroup_e(scalar_copy, "by128", "im", "im", 0)
+        for part in PARTS:
+            for j in range(PACK):
+                nc.scalar.copy(out=q_rows[part][:, 0, j, :], in_=acc0[part, j][:])
+        regroup_e(scalar_copy, "by128", "im", "im", 1)
+
+        def negate_and_quantise_im(g):
+            vector_negate(e_mx["by128", "neg_im"]["grouped"][:, g, :, :], e_mx["by128", "im"]["grouped"][:, g, :, :])
+            quantise(nc, e_mx["by128", "im"], g)
+            quantise(nc, e_mx["by128", "neg_im"], g)
+
+        negate_and_quantise_im(0)
+        regroup_e(vector_copy, "by128", "re", "re", 0)
+        regroup_q("re", 0)
+        quantise(nc, e_mx["by128", "re"], 0)
+        quantise(nc, q_mx["re"], 0)
+        regroup_q("im", 0)
+        regroup_e(vector_copy, "by128", "re", "re", 1)
+        quantise(nc, q_mx["im"], 0)
+        quantise(nc, e_mx["by128", "re"], 1)
+        negate_and_quantise_im(1)
+
+        for part in PARTS:
+            for j in range(PACK):
+                acc = banks.tile([P, POSITIONS], F32, name="acc", tag="acc")
+                for g in range(PASSES):
+                    for term in range(2):
+                        q_pass(acc, part, term, g, PACK + j)
+                nc.scalar.copy(out=q_rows[part][:, 1, j, :], in_=acc[:])
+            regroup_q(part, 1)
+            quantise(nc, q_mx[part], 1)
+
+        s_tiles = [(s_part, i) for s_part in PARTS for i in range(POSITIONS // M_TILE)]
+        s_acc = {key: banks.tile([P, POSITIONS], F32, name="acc", tag="acc") for key in s_tiles}
+        for g in range(PASSES):
+            for number, (s_part, i) in enumerate(s_tiles):
+                cols = slice(M_TILE * i, M_TILE * (i + 1))
+                for q_part in PARTS:
+                    e_operand = e_mx["by128", S_OPERAND[s_part, q_part]]
+                    nc.tensor.matmul_mx(
+                        out=s_acc[s_part, i][:],
+                        lhsT=e_operand["words"][:, g, cols].bitcast(FP8X4),
+                        lhsT_scale=e_operand["scales"][:, g, cols],
+                        rhs=q_mx[q_part]["words"][:, g, :].bitcast(FP8X4),
+                        rhs_scale=q_mx[q_part]["scales"][:, g, :],
+                        start=(g == 0 and q_part == "re"),
+                        stop=(g == PASSES - 1 and q_part == "im"),
+                    )
+                if g == PASSES - 1:
+                    s_rows = keep.tile([P, POSITIONS], F32, name="s_rows_%s_%d" % (s_part, i))
+                    if number % 2 == 0:
+                        nc.vector.tensor_copy(out=s_rows[:], in_=s_acc[s_part, i][:])
+                    else:
+                        nc.scalar.copy(out=s_rows[:], in_=s_acc[s_part, i][:])
+                    nc.sync.dma_start(out=s_dram[s_part][cols, :], in_=s_rows[:])

@@ -18,6 +18,7 @@ PASSES = CHANNELS // K_PASS
 M_TILE = 128
 HALF = PACK * M_TILE
 RUN = 4
+V_SHARE = 336
 BANKS = 8
 
 FLOPS = 2 * 4 * (CHANNELS * CHANNELS * POSITIONS + POSITIONS * CHANNELS * POSITIONS)
@@ -110,10 +111,10 @@ def tile_autoregressivelsa_pa_kernel(
         for w in PARTS:
             load_w_scales(w)
             load_w_words(w, 0, 0)
-        load_e("by4", "im", 0)
         load_e("by4", "re", 1)
-        for w in PARTS:
-            load_w_words(w, 1, 0)
+        load_w_words("re", 1, 0)
+        load_e("by4", "im", 0)
+        load_w_words("im", 1, 0)
         load_e("by4", "im", 1)
         load_e("by128", "im", 0)
         for g in range(PASSES):
@@ -153,23 +154,35 @@ def tile_autoregressivelsa_pa_kernel(
                 stop=(g == PASSES - 1 and term == 1),
             )
 
+        CLOSING = ("im", "re")
         acc0 = {
-            (part, j): banks.tile([P, POSITIONS], F32, name="acc", tag="acc") for part in PARTS for j in range(PACK)
+            (part, j): banks.tile([P, POSITIONS], F32, name="acc", tag="acc") for part in CLOSING for j in range(PACK)
         }
+
+        def regroup_shared(part, g):
+            grouped = e_mx["by4", part]["grouped"]
+            rows = e_rows["by4", part]
+            for copy, cols in ((vector_copy, slice(0, V_SHARE)), (scalar_copy, slice(V_SHARE, POSITIONS))):
+                dst, src = regroup_views(grouped[:, g, cols, :], rows[:, g, :, cols])
+                copy(dst, src)
+
         for g in range(PASSES):
-            regroup_e(vector_copy, "by4", "re", "re", g)
+            regroup_shared("re", g)
             quantise(nc, e_mx["by4", "re"], g)
-            regroup_e(scalar_copy, "by4", "im", "im", g)
-            regroup_e(vector_negate, "by4", "neg_im", "im", g)
-            quantise(nc, e_mx["by4", "neg_im"], g)
+            for part in PARTS:
+                for j in range(PACK):
+                    q_pass(acc0[part, j], part, 0, g, j)
+        for g in range(PASSES):
+            regroup_shared("im", g)
             quantise(nc, e_mx["by4", "im"], g)
-            for term in range(2):
-                for part in PARTS:
-                    for j in range(PACK):
-                        q_pass(acc0[part, j], part, term, g, j)
+            vector_negate(e_mx["by4", "neg_im"]["grouped"][:, g, :, :], e_mx["by4", "im"]["grouped"][:, g, :, :])
+            quantise(nc, e_mx["by4", "neg_im"], g)
+            for part in CLOSING:
+                for j in range(PACK):
+                    q_pass(acc0[part, j], part, 1, g, j)
 
         regroup_e(scalar_copy, "by128", "im", "im", 0)
-        for part in PARTS:
+        for part in CLOSING:
             for j in range(PACK):
                 nc.scalar.copy(out=q_rows[part][:, 0, j, :], in_=acc0[part, j][:])
         regroup_e(scalar_copy, "by128", "im", "im", 1)
@@ -181,12 +194,12 @@ def tile_autoregressivelsa_pa_kernel(
 
         negate_and_quantise_im(0)
         regroup_e(vector_copy, "by128", "re", "re", 0)
-        regroup_q("re", 0)
-        quantise(nc, e_mx["by128", "re"], 0)
-        quantise(nc, q_mx["re"], 0)
         regroup_q("im", 0)
-        regroup_e(vector_copy, "by128", "re", "re", 1)
+        quantise(nc, e_mx["by128", "re"], 0)
         quantise(nc, q_mx["im"], 0)
+        regroup_q("re", 0)
+        regroup_e(vector_copy, "by128", "re", "re", 1)
+        quantise(nc, q_mx["re"], 0)
         quantise(nc, e_mx["by128", "re"], 1)
         negate_and_quantise_im(1)
 

@@ -19,6 +19,7 @@ M_TILE = 128
 HALF = PACK * M_TILE
 RUN = 4
 V_SHARE = 336
+N_HALF = POSITIONS // 2
 BANKS = 8
 
 FLOPS = 2 * 4 * (CHANNELS * CHANNELS * POSITIONS + POSITIONS * CHANNELS * POSITIONS)
@@ -141,15 +142,15 @@ def tile_autoregressivelsa_pa_kernel(
             dst, src = regroup_views(q_mx[part]["grouped"][:, half, :, :], q_rows[part][:, half, :, :])
             nc.vector.tensor_copy(out=dst, in_=src)
 
-        def q_pass(acc, part, term, g, m):
+        def q_pass(acc, part, term, g, m, positions):
             w, operand = Q_TERMS[part][term]
             cols = slice(M_TILE * m, M_TILE * (m + 1))
             nc.tensor.matmul_mx(
-                out=acc[:],
+                out=acc,
                 lhsT=w_words[w][:, g, cols].bitcast(FP8X4),
                 lhsT_scale=w_scales[w_plane[w, g] : P, cols],
-                rhs=e_mx["by4", operand]["words"][:, g, :].bitcast(FP8X4),
-                rhs_scale=e_mx["by4", operand]["scales"][:, g, :],
+                rhs=e_mx["by4", operand]["words"][:, g, positions].bitcast(FP8X4),
+                rhs_scale=e_mx["by4", operand]["scales"][:, g, positions],
                 start=(g == 0 and term == 0),
                 stop=(g == PASSES - 1 and term == 1),
             )
@@ -171,7 +172,7 @@ def tile_autoregressivelsa_pa_kernel(
             quantise(nc, e_mx["by4", "re"], g)
             for part in PARTS:
                 for j in range(PACK):
-                    q_pass(acc0[part, j], part, 0, g, j)
+                    q_pass(acc0[part, j][:], part, 0, g, j, slice(0, POSITIONS))
         for g in range(PASSES):
             regroup_shared("im", g)
             quantise(nc, e_mx["by4", "im"], g)
@@ -179,7 +180,7 @@ def tile_autoregressivelsa_pa_kernel(
             quantise(nc, e_mx["by4", "neg_im"], g)
             for part in CLOSING:
                 for j in range(PACK):
-                    q_pass(acc0[part, j], part, 1, g, j)
+                    q_pass(acc0[part, j][:], part, 1, g, j, slice(0, POSITIONS))
 
         regroup_e(scalar_copy, "by128", "im", "im", 0)
         for part in CLOSING:
@@ -204,13 +205,18 @@ def tile_autoregressivelsa_pa_kernel(
         negate_and_quantise_im(1)
 
         for part in PARTS:
-            for j in range(PACK):
-                acc = banks.tile([P, POSITIONS], F32, name="acc", tag="acc")
-                for g in range(PASSES):
-                    for term in range(2):
-                        q_pass(acc, part, term, g, PACK + j)
-                nc.scalar.copy(out=q_rows[part][:, 1, j, :], in_=acc[:])
-            regroup_q(part, 1)
+            for c in range(2):
+                cols = slice(N_HALF * c, N_HALF * (c + 1))
+                for pair in range(PACK // 2):
+                    acc = banks.tile([P, 2, N_HALF], F32, name="acc", tag="acc")
+                    for k in range(2):
+                        for g in range(PASSES):
+                            for term in range(2):
+                                q_pass(acc[:, k, :], part, term, g, PACK + 2 * pair + k, cols)
+                    nc.scalar.copy(
+                        out=q_mx[part]["grouped"][:, 1, cols, 2 * pair : 2 * pair + 2],
+                        in_=acc[:].rearrange("p k n -> p n k"),
+                    )
             quantise(nc, q_mx[part], 1)
 
         s_tiles = [(s_part, i) for s_part in PARTS for i in range(POSITIONS // M_TILE)]

@@ -20,6 +20,9 @@ HALF = PACK * M_TILE
 RUN = 4
 V_SHARE = 336
 N_HALF = POSITIONS // 2
+S_LEAD = 5
+WARM_ZERO = 8
+WARM_DATA = 3
 BANKS = 8
 
 FLOPS = 2 * 4 * (CHANNELS * CHANNELS * POSITIONS + POSITIONS * CHANNELS * POSITIONS)
@@ -108,6 +111,11 @@ def tile_autoregressivelsa_pa_kernel(
                 )
 
         nc.vector.memset(w_scales[:].bitcast(I32), 0)
+        warm_in = keep.tile([P, POSITIONS], BF16, name="warm_in")
+        nc.gpsimd.memset(warm_in[:], 0.0)
+        warm_out = banks.tile([P, POSITIONS], F32, name="acc", tag="acc")
+        for unused in range(WARM_ZERO):
+            nc.tensor.matmul(out=warm_out[:], lhsT=warm_in[:, 0:M_TILE], rhs=warm_in[:], start=True, stop=True)
         load_e("by4", "re", 0)
         for w in PARTS:
             load_w_scales(w)
@@ -153,6 +161,15 @@ def tile_autoregressivelsa_pa_kernel(
                 rhs_scale=e_mx["by4", operand]["scales"][:, g, positions],
                 start=(g == 0 and term == 0),
                 stop=(g == PASSES - 1 and term == 1),
+            )
+
+        for unused in range(WARM_DATA):
+            nc.tensor.matmul(
+                out=warm_out[:],
+                lhsT=e_rows["by4", "re"][:, 0, 0, 0:M_TILE],
+                rhs=e_rows["by4", "re"][:, 0, 0, :],
+                start=True,
+                stop=True,
             )
 
         CLOSING = ("im", "re")
@@ -217,28 +234,52 @@ def tile_autoregressivelsa_pa_kernel(
                         out=q_mx[part]["grouped"][:, 1, cols, 2 * pair : 2 * pair + 2],
                         in_=acc[:].rearrange("p k n -> p n k"),
                     )
-            quantise(nc, q_mx[part], 1)
+                nc.vector.quantize_mx(
+                    out=q_mx[part]["words"][:, 1, cols].bitcast(FP8X4),
+                    scales=q_mx[part]["scales"][:, 1, cols],
+                    in_=q_mx[part]["grouped"][:, 1, cols, :].rearrange("p w j -> p (w j)"),
+                )
 
         s_tiles = [(s_part, i) for s_part in PARTS for i in range(POSITIONS // M_TILE)]
-        s_acc = {key: banks.tile([P, POSITIONS], F32, name="acc", tag="acc") for key in s_tiles}
-        for g in range(PASSES):
-            for number, (s_part, i) in enumerate(s_tiles):
-                cols = slice(M_TILE * i, M_TILE * (i + 1))
-                for q_part in PARTS:
-                    e_operand = e_mx["by128", S_OPERAND[s_part, q_part]]
-                    nc.tensor.matmul_mx(
-                        out=s_acc[s_part, i][:],
-                        lhsT=e_operand["words"][:, g, cols].bitcast(FP8X4),
-                        lhsT_scale=e_operand["scales"][:, g, cols],
-                        rhs=q_mx[q_part]["words"][:, g, :].bitcast(FP8X4),
-                        rhs_scale=q_mx[q_part]["scales"][:, g, :],
-                        start=(g == 0 and q_part == "re"),
-                        stop=(g == PASSES - 1 and q_part == "im"),
-                    )
-                if g == PASSES - 1:
-                    s_rows = keep.tile([P, POSITIONS], F32, name="s_rows_%s_%d" % (s_part, i))
-                    if number % 2 == 0:
-                        nc.vector.tensor_copy(out=s_rows[:], in_=s_acc[s_part, i][:])
-                    else:
-                        nc.scalar.copy(out=s_rows[:], in_=s_acc[s_part, i][:])
-                    nc.sync.dma_start(out=s_dram[s_part][cols, :], in_=s_rows[:])
+
+        def s_passes(acc, s_part, i, g, q_cols):
+            rows = slice(M_TILE * i, M_TILE * (i + 1))
+            for q_part in PARTS:
+                e_operand = e_mx["by128", S_OPERAND[s_part, q_part]]
+                nc.tensor.matmul_mx(
+                    out=acc[:],
+                    lhsT=e_operand["words"][:, g, rows].bitcast(FP8X4),
+                    lhsT_scale=e_operand["scales"][:, g, rows],
+                    rhs=q_mx[q_part]["words"][:, g, q_cols].bitcast(FP8X4),
+                    rhs_scale=q_mx[q_part]["scales"][:, g, q_cols],
+                    start=(g == 0 and q_part == "re"),
+                    stop=(g == PASSES - 1 and q_part == "im"),
+                )
+
+        def s_out(acc, s_part, i, q_cols, on_vector):
+            width = q_cols.stop - q_cols.start
+            s_rows = keep.tile([P, width], F32, name="s_rows_%s_%d_%d" % (s_part, i, q_cols.start))
+            if on_vector:
+                nc.vector.tensor_copy(out=s_rows[:], in_=acc[:])
+            else:
+                nc.scalar.copy(out=s_rows[:], in_=acc[:])
+            nc.sync.dma_start(out=s_dram[s_part][M_TILE * i : M_TILE * (i + 1), q_cols], in_=s_rows[:])
+
+        whole = slice(0, POSITIONS)
+        s_acc = {}
+        for s_part, i in s_tiles[:S_LEAD]:
+            s_acc[s_part, i] = banks.tile([P, POSITIONS], F32, name="acc", tag="acc")
+            s_passes(s_acc[s_part, i], s_part, i, 0, whole)
+        for number, (s_part, i) in enumerate(s_tiles[:-1]):
+            if number >= S_LEAD:
+                s_acc[s_part, i] = banks.tile([P, POSITIONS], F32, name="acc", tag="acc")
+                s_passes(s_acc[s_part, i], s_part, i, 0, whole)
+            s_passes(s_acc[s_part, i], s_part, i, 1, whole)
+            s_out(s_acc[s_part, i], s_part, i, whole, number % 2 == 0)
+        s_part, i = s_tiles[-1]
+        for c in range(2):
+            q_cols = slice(N_HALF * c, N_HALF * (c + 1))
+            acc = banks.tile([P, N_HALF], F32, name="acc", tag="acc")
+            for g in range(PASSES):
+                s_passes(acc, s_part, i, g, q_cols)
+            s_out(acc, s_part, i, q_cols, c == 1)

@@ -71,7 +71,7 @@ def tile_autoregressivelsa_pa_kernel(
         ctx.enter_context(tc.manual_schedule())
 
         w_words = {w: keep.tile([P, PASSES, CHANNELS], U32, name="w_words_" + w, align_bytes=64) for w in PARTS}
-        w_scales = keep.tile([P, CHANNELS], U8, name="w_scales", align_bytes=64)
+        w_scales = keep.tile([P, len(PARTS), CHANNELS], U8, name="w_scales", align_bytes=64)
         w_plane = {(w, g): PACK * (PASSES * PARTS.index(w) + g) for w in PARTS for g in range(PASSES)}
 
         e_rows = {}
@@ -105,8 +105,9 @@ def tile_autoregressivelsa_pa_kernel(
         def load_w_scales(w):
             first = w_plane[w, 0]
             for quadrant in range(4):
+                rows = slice(32 * quadrant + first, 32 * quadrant + first + PACK * PASSES)
                 nc.sync.dma_start(
-                    out=w_scales[32 * quadrant + first : 32 * quadrant + first + PACK * PASSES, :].bitcast(I32),
+                    out=w_scales[rows, PARTS.index(w), :].bitcast(I32),
                     in_=w_scales_dram[w][:, 4 * quadrant : 4 * quadrant + 4, :].bitcast(I32),
                 )
 
@@ -156,7 +157,7 @@ def tile_autoregressivelsa_pa_kernel(
             nc.tensor.matmul_mx(
                 out=acc,
                 lhsT=w_words[w][:, g, cols].bitcast(FP8X4),
-                lhsT_scale=w_scales[w_plane[w, g] : P, cols],
+                lhsT_scale=w_scales[w_plane[w, g] : P, PARTS.index(w), cols],
                 rhs=e_mx["by4", operand]["words"][:, g, positions].bitcast(FP8X4),
                 rhs_scale=e_mx["by4", operand]["scales"][:, g, positions],
                 start=(g == 0 and term == 0),

@@ -118,14 +118,15 @@ def tile_autoregressivelsa_pa_kernel(
         for unused in range(WARM_ZERO):
             nc.tensor.matmul(out=warm_out[:], lhsT=warm_in[:, 0:M_TILE], rhs=warm_in[:], start=True, stop=True)
         load_e("by4", "re", 0)
-        for w in PARTS:
-            load_w_scales(w)
-            load_w_words(w, 0, 0)
-        load_e("by4", "re", 1)
-        load_w_words("re", 1, 0)
+        load_w_scales("re")
+        load_w_words("re", 0, 0)
         load_e("by4", "im", 0)
-        load_w_words("im", 1, 0)
+        load_w_scales("im")
+        load_w_words("im", 0, 0)
+        load_e("by4", "re", 1)
         load_e("by4", "im", 1)
+        load_w_words("re", 1, 0)
+        load_w_words("im", 1, 0)
         load_e("by128", "im", 0)
         for g in range(PASSES):
             for w in PARTS:
@@ -191,7 +192,6 @@ def tile_autoregressivelsa_pa_kernel(
             for part in PARTS:
                 for j in range(PACK):
                     q_pass(acc0[part, j][:], part, 0, g, j, slice(0, POSITIONS))
-        for g in range(PASSES):
             regroup_shared("im", g)
             quantise(nc, e_mx["by4", "im"], g)
             vector_negate(e_mx["by4", "neg_im"]["grouped"][:, g, :, :], e_mx["by4", "im"]["grouped"][:, g, :, :])

@@ -20,7 +20,7 @@ HALF = PACK * M_TILE
 RUN = 4
 V_SHARE = 336
 N_HALF = POSITIONS // 2
-S_LEAD = 5
+S_LEAD = 7
 WARM_ZERO = 8
 WARM_DATA = 3
 BANKS = 8

from contextlib import ExitStack

import concourse.mybir as mybir

FP8X4 = mybir.dt.float8_e4m3fn_x4
BF16 = mybir.dt.bfloat16
F32 = mybir.dt.float32
I32 = mybir.dt.int32
U32 = mybir.dt.uint32
U8 = mybir.dt.uint8

P = 128
PACK = 4
K_PASS = P * PACK
CHANNELS = 1024
POSITIONS = 512
PASSES = CHANNELS // K_PASS
M_TILE = 128
HALF = PACK * M_TILE
RUN = 4
V_SHARE = 336
N_HALF = POSITIONS // 2
S_LEAD = 7
WARM_ZERO = 8
WARM_DATA = 3
BANKS = 8

FLOPS = 2 * 4 * (CHANNELS * CHANNELS * POSITIONS + POSITIONS * CHANNELS * POSITIONS)

PARTS = ("re", "im")

Q_TERMS = {"re": (("re", "re"), ("im", "neg_im")), "im": (("im", "re"), ("re", "im"))}
S_OPERAND = {("re", "re"): "re", ("re", "im"): "im", ("im", "re"): "neg_im", ("im", "im"): "re"}


def mx_operand(pool, name, passes, columns):
    return {
        "grouped": pool.tile([P, passes, columns, PACK], BF16, name=name + "_grouped", align_bytes=64),
        "words": pool.tile([P, passes, columns], U32, name=name + "_words", align_bytes=64),
        "scales": pool.tile([P, passes, columns], U8, name=name + "_scales", align_bytes=64),
    }


def regroup_views(grouped, rows):
    return (
        grouped.rearrange("p (c i) j -> p c j i", i=RUN),
        rows.rearrange("p j (c i) -> p c j i", i=RUN),
    )


def quantise(nc, operand, g):
    nc.vector.quantize_mx(
        out=operand["words"][:, g, :].bitcast(FP8X4),
        scales=operand["scales"][:, g, :],
        in_=operand["grouped"][:, g, :, :].rearrange("p w j -> p (w j)"),
    )


def tile_autoregressivelsa_pa_kernel(
    tc, E_re, E_im, WKQ_re_words, WKQ_re_scales, WKQ_im_words, WKQ_im_scales, out_0, out_1
):
    nc = tc.nc
    e_dram = {"re": E_re.flatten_outer_dims(), "im": E_im.flatten_outer_dims()}
    w_words_dram = {"re": WKQ_re_words, "im": WKQ_im_words}
    w_scales_dram = {"re": WKQ_re_scales, "im": WKQ_im_scales}
    s_dram = {"re": out_0.flatten_outer_dims(), "im": out_1.flatten_outer_dims()}

    with ExitStack() as ctx:
        keep = ctx.enter_context(tc.tile_pool(name="keep", bufs=1))
        banks = ctx.enter_context(tc.psum_pool(name="banks", bufs=BANKS))
        ctx.enter_context(tc.manual_schedule())

        w_words = {w: keep.tile([P, PASSES, CHANNELS], U32, name="w_words_" + w, align_bytes=64) for w in PARTS}
        w_scales = keep.tile([P, len(PARTS), CHANNELS], U8, name="w_scales", align_bytes=64)
        w_plane = {(w, g): PACK * (PASSES * PARTS.index(w) + g) for w in PARTS for g in range(PASSES)}

        e_rows = {}
        e_mx = {}
        for order in ("by4", "by128"):
            for part in PARTS:
                e_rows[order, part] = keep.tile(
                    [P, PASSES, PACK, POSITIONS], BF16, name="e_rows_%s_%s" % (order, part)
                )
            for operand in ("re", "im", "neg_im"):
                e_mx[order, operand] = mx_operand(keep, "e_%s_%s" % (order, operand), PASSES, POSITIONS)
        q_rows = {part: keep.tile([P, PASSES, PACK, POSITIONS], BF16, name="q_rows_" + part) for part in PARTS}
        q_mx = {part: mx_operand(keep, "q_" + part, PASSES, POSITIONS) for part in PARTS}

        def load_e(order, part, g):
            rows = e_dram[part][K_PASS * g : K_PASS * (g + 1), :]
            if order == "by4":
                view = rows.rearrange("(p j) t -> p j t", j=PACK)
            else:
                view = rows.rearrange("(j p) t -> p j t", p=P)
            nc.sync.dma_start(out=e_rows[order, part][:, g, :, :], in_=view)

        def load_w_words(w, g, half):
            cols = slice(HALF * half, HALF * (half + 1))
            byte_cols = slice(PACK * HALF * half, PACK * HALF * (half + 1))
            nc.sync.dma_start(
                out=w_words[w][:, g, cols].bitcast(I32),
                in_=w_words_dram[w][g].rearrange("p n t -> p (n t)")[:, byte_cols].bitcast(I32),
            )

        def load_w_scales(w):
            first = w_plane[w, 0]
            for quadrant in range(4):
                rows = slice(32 * quadrant + first, 32 * quadrant + first + PACK * PASSES)
                nc.sync.dma_start(
                    out=w_scales[rows, PARTS.index(w), :].bitcast(I32),
                    in_=w_scales_dram[w][:, 4 * quadrant : 4 * quadrant + 4, :].bitcast(I32),
                )

        nc.vector.memset(w_scales[:].bitcast(I32), 0)
        warm_in = keep.tile([P, POSITIONS], BF16, name="warm_in")
        nc.gpsimd.memset(warm_in[:], 0.0)
        warm_out = banks.tile([P, POSITIONS], F32, name="acc", tag="acc")
        for unused in range(WARM_ZERO):
            nc.tensor.matmul(out=warm_out[:], lhsT=warm_in[:, 0:M_TILE], rhs=warm_in[:], start=True, stop=True)
        load_e("by4", "re", 0)
        load_w_scales("re")
        load_w_words("re", 0, 0)
        load_e("by4", "im", 0)
        load_w_scales("im")
        load_w_words("im", 0, 0)
        load_e("by4", "re", 1)
        load_e("by4", "im", 1)
        load_w_words("re", 1, 0)
        load_w_words("im", 1, 0)
        load_e("by128", "im", 0)
        for g in range(PASSES):
            for w in PARTS:
                load_w_words(w, g, 1)
        load_e("by128", "re", 0)
        load_e("by128", "re", 1)
        load_e("by128", "im", 1)

        def regroup_e(copy, order, operand, part, g):
            dst, src = regroup_views(e_mx[order, operand]["grouped"][:, g, :, :], e_rows[order, part][:, g, :, :])
            copy(dst, src)

        def vector_copy(dst, src):
            nc.vector.tensor_copy(out=dst, in_=src)

        def vector_negate(dst, src):
            nc.vector.tensor_scalar_mul(out=dst, in0=src, scalar1=-1.0)

        def scalar_copy(dst, src):
            nc.scalar.copy(out=dst, in_=src)

        def regroup_q(part, half):
            dst, src = regroup_views(q_mx[part]["grouped"][:, half, :, :], q_rows[part][:, half, :, :])
            nc.vector.tensor_copy(out=dst, in_=src)

        def q_pass(acc, part, term, g, m, positions):
            w, operand = Q_TERMS[part][term]
            cols = slice(M_TILE * m, M_TILE * (m + 1))
            nc.tensor.matmul_mx(
                out=acc,
                lhsT=w_words[w][:, g, cols].bitcast(FP8X4),
                lhsT_scale=w_scales[w_plane[w, g] : P, PARTS.index(w), cols],
                rhs=e_mx["by4", operand]["words"][:, g, positions].bitcast(FP8X4),
                rhs_scale=e_mx["by4", operand]["scales"][:, g, positions],
                start=(g == 0 and term == 0),
                stop=(g == PASSES - 1 and term == 1),
            )

        for unused in range(WARM_DATA):
            nc.tensor.matmul(
                out=warm_out[:],
                lhsT=e_rows["by4", "re"][:, 0, 0, 0:M_TILE],
                rhs=e_rows["by4", "re"][:, 0, 0, :],
                start=True,
                stop=True,
            )

        CLOSING = ("im", "re")
        acc0 = {
            (part, j): banks.tile([P, POSITIONS], F32, name="acc", tag="acc") for part in CLOSING for j in range(PACK)
        }

        def regroup_shared(part, g):
            grouped = e_mx["by4", part]["grouped"]
            rows = e_rows["by4", part]
            for copy, cols in ((vector_copy, slice(0, V_SHARE)), (scalar_copy, slice(V_SHARE, POSITIONS))):
                dst, src = regroup_views(grouped[:, g, cols, :], rows[:, g, :, cols])
                copy(dst, src)

        for g in range(PASSES):
            regroup_shared("re", g)
            quantise(nc, e_mx["by4", "re"], g)
            for part in PARTS:
                for j in range(PACK):
                    q_pass(acc0[part, j][:], part, 0, g, j, slice(0, POSITIONS))
            regroup_shared("im", g)
            quantise(nc, e_mx["by4", "im"], g)
            vector_negate(e_mx["by4", "neg_im"]["grouped"][:, g, :, :], e_mx["by4", "im"]["grouped"][:, g, :, :])
            quantise(nc, e_mx["by4", "neg_im"], g)
            for part in CLOSING:
                for j in range(PACK):
                    q_pass(acc0[part, j][:], part, 1, g, j, slice(0, POSITIONS))

        regroup_e(scalar_copy, "by128", "im", "im", 0)
        for part in CLOSING:
            for j in range(PACK):
                nc.scalar.copy(out=q_rows[part][:, 0, j, :], in_=acc0[part, j][:])
        regroup_e(scalar_copy, "by128", "im", "im", 1)

        def negate_and_quantise_im(g):
            vector_negate(e_mx["by128", "neg_im"]["grouped"][:, g, :, :], e_mx["by128", "im"]["grouped"][:, g, :, :])
            quantise(nc, e_mx["by128", "im"], g)
            quantise(nc, e_mx["by128", "neg_im"], g)

        negate_and_quantise_im(0)
        regroup_e(vector_copy, "by128", "re", "re", 0)
        regroup_q("im", 0)
        quantise(nc, e_mx["by128", "re"], 0)
        quantise(nc, q_mx["im"], 0)
        regroup_q("re", 0)
        regroup_e(vector_copy, "by128", "re", "re", 1)
        quantise(nc, q_mx["re"], 0)
        quantise(nc, e_mx["by128", "re"], 1)
        negate_and_quantise_im(1)

        for part in PARTS:
            for c in range(2):
                cols = slice(N_HALF * c, N_HALF * (c + 1))
                for pair in range(PACK // 2):
                    acc = banks.tile([P, 2, N_HALF], F32, name="acc", tag="acc")
                    for k in range(2):
                        for g in range(PASSES):
                            for term in range(2):
                                q_pass(acc[:, k, :], part, term, g, PACK + 2 * pair + k, cols)
                    nc.scalar.copy(
                        out=q_mx[part]["grouped"][:, 1, cols, 2 * pair : 2 * pair + 2],
                        in_=acc[:].rearrange("p k n -> p n k"),
                    )
                nc.vector.quantize_mx(
                    out=q_mx[part]["words"][:, 1, cols].bitcast(FP8X4),
                    scales=q_mx[part]["scales"][:, 1, cols],
                    in_=q_mx[part]["grouped"][:, 1, cols, :].rearrange("p w j -> p (w j)"),
                )

        s_tiles = [(s_part, i) for s_part in PARTS for i in range(POSITIONS // M_TILE)]

        def s_passes(acc, s_part, i, g, q_cols):
            rows = slice(M_TILE * i, M_TILE * (i + 1))
            for q_part in PARTS:
                e_operand = e_mx["by128", S_OPERAND[s_part, q_part]]
                nc.tensor.matmul_mx(
                    out=acc[:],
                    lhsT=e_operand["words"][:, g, rows].bitcast(FP8X4),
                    lhsT_scale=e_operand["scales"][:, g, rows],
                    rhs=q_mx[q_part]["words"][:, g, q_cols].bitcast(FP8X4),
                    rhs_scale=q_mx[q_part]["scales"][:, g, q_cols],
                    start=(g == 0 and q_part == "re"),
                    stop=(g == PASSES - 1 and q_part == "im"),
                )

        def s_out(acc, s_part, i, q_cols, on_vector):
            width = q_cols.stop - q_cols.start
            s_rows = keep.tile([P, width], F32, name="s_rows_%s_%d_%d" % (s_part, i, q_cols.start))
            if on_vector:
                nc.vector.tensor_copy(out=s_rows[:], in_=acc[:])
            else:
                nc.scalar.copy(out=s_rows[:], in_=acc[:])
            nc.sync.dma_start(out=s_dram[s_part][M_TILE * i : M_TILE * (i + 1), q_cols], in_=s_rows[:])

        whole = slice(0, POSITIONS)
        s_acc = {}
        for s_part, i in s_tiles[:S_LEAD]:
            s_acc[s_part, i] = banks.tile([P, POSITIONS], F32, name="acc", tag="acc")
            s_passes(s_acc[s_part, i], s_part, i, 0, whole)
        for number, (s_part, i) in enumerate(s_tiles[:-1]):
            if number >= S_LEAD:
                s_acc[s_part, i] = banks.tile([P, POSITIONS], F32, name="acc", tag="acc")
                s_passes(s_acc[s_part, i], s_part, i, 0, whole)
            s_passes(s_acc[s_part, i], s_part, i, 1, whole)
            s_out(s_acc[s_part, i], s_part, i, whole, number % 2 == 0)
        s_part, i = s_tiles[-1]
        for c in range(2):
            q_cols = slice(N_HALF * c, N_HALF * (c + 1))
            acc = banks.tile([P, N_HALF], F32, name="acc", tag="acc")
            for g in range(PASSES):
                s_passes(acc, s_part, i, g, q_cols)
            s_out(acc, s_part, i, q_cols, c == 1)
